import numpy as np
import ml_dtypes


def mxq(x, axis, fmt="e4m3"):
    dtype, down = {"e4m3": (ml_dtypes.float8_e4m3fn, 7), "e5m2": (ml_dtypes.float8_e5m2, 14)}[fmt]
    v = np.moveaxis(np.asarray(x, np.float32).astype(ml_dtypes.bfloat16).astype(np.float64), axis, -1)
    blocks = v.reshape(v.shape[:-1] + (-1, 32))
    amax = np.abs(blocks).max(-1, keepdims=True)
    byte = np.maximum(np.where(amax > 0, np.frexp(amax)[1] - 1 + 127, 0) - down, 1)
    scale = np.exp2(byte - 127.0)
    codes = (blocks / scale).astype(np.float32).astype(dtype).astype(np.float64)
    return np.moveaxis((codes * scale).reshape(v.shape), -1, axis)


WIDE = False


def mx_kscale(k):
    if not WIDE:
        return np.ones(k)
    levels = np.array([10, -10, 5, -5, 0])
    if k % 512:
        return np.exp2(np.random.permutation(np.resize(levels, k // 32))).repeat(32)
    a = np.empty((k // 512, 16))
    for p in range(k // 512):
        a[p, :8] = np.random.permutation(np.resize(levels, 8))
        for g in range(8):
            far = levels[np.abs(levels - a[p, g]) >= 10]
            a[p, g + 8] = far[np.random.randint(len(far))]
    return np.exp2(a.ravel()).repeat(32)


BF16 = ml_dtypes.bfloat16


def bf(x):
    return np.asarray(x, np.float32).astype(BF16)


def f64(x):
    return np.asarray(x).astype(np.float64)


B, I, H, S = 512, 512, 1024, 4096
LAM_DIRECT = 1.0
LAM_SPARSE = 1.0
SIG = 1.0
EPS = 0.0001
G = 1.5


def setup_inputs():
    si, sh, ss = mx_kscale(I), mx_kscale(H), mx_kscale(S)
    z = np.random.standard_normal((B, S)) * G * np.sqrt(2.0)
    e = np.exp(z - z.max(axis=1, keepdims=True))
    sy = e / e.sum(axis=1, keepdims=True)
    return {"x": bf(np.random.standard_normal((B, I)) * si),
            "hx": bf(np.random.standard_normal((B, H)) * sh),
            "sy": bf(sy * ss),
            "internal": bf(np.random.standard_normal((B, H))),
            "W_ih": bf(np.random.standard_normal((H, I)) * 0.7 / np.sqrt(I) / si),
            "W_hh": bf(np.random.standard_normal((H, H)) * 0.7 / np.sqrt(H) / sh),
            "W_sh": bf(np.random.standard_normal((H, S)) * 3.0 / ss),
            "mu": bf(np.random.standard_normal(H) * 0.3)}


def reference(x, hx, sy, internal, W_ih, W_hh, W_sh, mu):
    direct = mxq(f64(x), 1, "e4m3") @ mxq(f64(W_ih).T, 0, "e4m3")
    recur = mxq(f64(hx), 1, "e4m3") @ mxq(f64(W_hh).T, 0, "e4m3")
    sparse = mxq(f64(sy), 1, "e4m3") @ mxq(f64(W_sh).T, 0, "e4m3")
    pre = LAM_DIRECT * direct + recur + LAM_SPARSE * sparse
    m = pre.mean(-1, keepdims=True)
    sd = np.sqrt(((pre - m) ** 2).mean(-1, keepdims=True)) + EPS
    ln = (pre - m) / sd * SIG + f64(mu)
    return np.maximum(ln + f64(internal), 0.0)

@@ -1,0 +1,205 @@
+from contextlib import ExitStack
+
+import concourse.mybir as mybir
+from concourse.masks import make_identity
+
+F32 = mybir.dt.float32
+BF16 = mybir.dt.bfloat16
+U32 = mybir.dt.uint32
+U8 = mybir.dt.uint8
+FP8X4 = mybir.dt.float8_e4m3fn_x4
+ALU = mybir.AluOpType
+ACT = mybir.ActivationFunctionType
+
+P = 128
+PACK = 4
+K_PASS = P * PACK
+PASS_WORDS = K_PASS // 2
+B, H = 512, 1024
+B_TILES = B // P
+H_HALF = 512
+SLAB_ROWS = 512
+ROW_TILES = SLAB_ROWS // P
+K_TOTAL = 512 + 1024 + 4096
+PASSES = K_TOTAL // K_PASS
+K_CHUNK = 2 * K_PASS
+RAW_BUFS = 8
+LAG = 3
+EPS = 0.0001
+
+FLOPS = 2 * B * H * K_TOTAL
+
+
+def tile_sparsegatedrnncell_pb_kernel(tc, x, hx, sy, internal, W_ih, W_hh, W_sh, mu, out):
+    nc = tc.nc
+    with ExitStack() as ctx:
+        const = ctx.enter_context(tc.tile_pool(name="const", bufs=1))
+        keep = ctx.enter_context(tc.tile_pool(name="keep", bufs=1))
+        raw_pool = ctx.enter_context(tc.tile_pool(name="raw_pool", bufs=RAW_BUFS))
+        stage = ctx.enter_context(tc.tile_pool(name="stage", bufs=4))
+        banks = ctx.enter_context(tc.psum_pool(name="banks", bufs=4))
+        sums = ctx.enter_context(tc.psum_pool(name="sums", bufs=4))
+        ctx.enter_context(tc.manual_schedule())
+
+        chunks = []
+        where_is = []
+        for act, weight in ((x, W_ih), (hx, W_hh), (sy, W_sh)):
+            for k0 in range(0, act.shape[1], K_CHUNK):
+                width = min(K_CHUNK, act.shape[1] - k0)
+                for local in range(width // K_PASS):
+                    where_is.append((len(chunks), local, width, local == width // K_PASS - 1))
+                chunks.append((act, weight, k0, width))
+        loads = []
+        for n, (act, weight, k0, width) in enumerate(chunks):
+            loads.append((("act", n), act, 0, k0, width))
+            loads.append((("w", 0, n), weight, 0, k0, width))
+        for n, (act, weight, k0, width) in enumerate(chunks):
+            loads.append((("w", 1, n), weight, H_HALF, k0, width))
+        raw = {}
+
+        def issue_loads(count):
+            for key, source, row0, k0, width in loads[len(raw) : len(raw) + count]:
+                rows = raw_pool.tile([P, ROW_TILES * K_CHUNK], BF16, name="rows", tag="rows")
+                nc.sync.dma_start(
+                    out=rows[:, 0 : ROW_TILES * width].rearrange("p (j k) -> p j k", j=ROW_TILES),
+                    in_=source[row0 : row0 + SLAB_ROWS, k0 : k0 + width].rearrange("(j p) k -> p j k", p=P),
+                )
+                raw[key] = rows
+
+        mu_rows = const.tile([P, H], BF16)
+        nc.vector.memset(mu_rows[:], 0.0)
+        nc.sync.dma_start(out=mu_rows[0:1, :], in_=mu.rearrange("(o h) -> o h", o=1))
+        issue_loads(RAW_BUFS)
+        internal_sb = const.tile([P, B_TILES, H], BF16)
+        nc.sync.dma_start(out=internal_sb[:], in_=internal.rearrange("(t p) h -> p t h", p=P))
+
+        ones = const.tile([P, P], BF16)
+        nc.vector.memset(ones[:], 1.0)
+        warm = const.tile([P, 1], F32)
+        nc.vector.memset(warm[:], 1.0)
+        nc.scalar.activation(out=warm[:], in_=warm[:], func=ACT.Sqrt)
+        ident = const.tile([P, P], F32)
+        make_identity(nc, ident[:])
+
+        mu_all = const.tile([P, H], BF16)
+        for half in range(2):
+            cols = slice(half * H_HALF, (half + 1) * H_HALF)
+            spread = banks.tile([P, H_HALF], F32, tag="bank")
+            nc.tensor.matmul(out=spread[:], lhsT=ones[:], rhs=mu_rows[:, cols], start=True, stop=True)
+            nc.vector.tensor_copy(out=mu_all[:, cols], in_=spread[:])
+
+        a_codes = keep.tile([P, PASSES, B], U32, align_bytes=64)
+        a_scales = keep.tile([P, PASSES, B], U8, align_bytes=64)
+        w_codes = keep.tile([P, PASSES, H], U32, align_bytes=64)
+        w_scales = keep.tile([P, PASSES, H], U8, align_bytes=64)
+
+        def transpose_slab(rows, width, local):
+            words = rows[:].bitcast(F32)
+            grouped = stage.tile([P, SLAB_ROWS * PACK], BF16, align_bytes=64, tag="grouped")
+            grouped_words = grouped[:].bitcast(F32).rearrange("p (j r u) -> p j r u", j=ROW_TILES, u=2)
+            for pair in range(ROW_TILES // 2):
+                bank = banks.tile([P, 2, 2, P], F32, tag="bank")
+                for j in range(2):
+                    for u in range(2):
+                        first = (2 * pair + j) * (width // 2) + local * PASS_WORDS
+                        nc.tensor.transpose(bank[:, j, u, :], words[:, first + u : first + PASS_WORDS : 2], ident[:])
+                nc.scalar.copy(
+                    out=grouped_words[:, 2 * pair : 2 * pair + 2, :, :],
+                    in_=bank[:].rearrange("p j u r -> p j r u"),
+                )
+            return grouped
+
+        def quantise(grouped, codes, scales):
+            nc.vector.quantize_mx(out=codes.bitcast(FP8X4), scales=scales, in_=grouped[:])
+
+        def mx_passes(acc, row_tiles, half, pass_list):
+            h_cols = slice(half * H_HALF, (half + 1) * H_HALF)
+            for t in row_tiles:
+                b_cols = slice(t * P, (t + 1) * P)
+                for c in pass_list:
+                    nc.tensor.matmul_mx(
+                        out=acc[t][:],
+                        lhsT=a_codes[:, c, b_cols].bitcast(FP8X4),
+                        lhsT_scale=a_scales[:, c, b_cols],
+                        rhs=w_codes[:, c, h_cols].bitcast(FP8X4),
+                        rhs_scale=w_scales[:, c, h_cols],
+                        start=(c == 0),
+                        stop=(c == PASSES - 1),
+                    )
+
+        all_tiles = range(B_TILES)
+        first_cols = slice(0, H_HALF)
+        second_cols = slice(H_HALF, H)
+        slabs = []
+        runs = []
+        for c in range(PASSES):
+            n = where_is[c][0]
+            slabs.append((("act", n), c, a_codes[:, c, :], a_scales[:, c, :]))
+            slabs.append((("w", 0, n), c, w_codes[:, c, first_cols], w_scales[:, c, first_cols]))
+            runs.append((0, c, (0, 1)))
+            runs.append((0, c, (2, 3)))
+        part1_slabs = len(slabs)
+        for c in range(PASSES):
+            n = where_is[c][0]
+            slabs.append((("w", 1, n), c, w_codes[:, c, second_cols], w_scales[:, c, second_cols]))
+            runs.append((1, c, (0, 1)))
+
+        acc = {0: [sums.tile([P, H_HALF], F32, name="acc_first%d" % t, tag="acc") for t in all_tiles], 1: []}
+        result = [keep.tile([P, H], F32, name="result%d" % t) for t in all_tiles]
+        pre_first = [keep.tile([P, H_HALF], F32, name="pre_first%d" % t) for t in all_tiles]
+        stats = [keep.tile([P, 2, 6], F32, name="stats%d" % t) for t in all_tiles]
+        for i in range(len(slabs) + LAG):
+            if i < len(slabs):
+                key, c, codes, scales = slabs[i]
+                n, local, width, last_of_chunk = where_is[c]
+                grouped = transpose_slab(raw[key], width, local)
+                if last_of_chunk and len(raw) < len(loads):
+                    issue_loads(1)
+            if i >= LAG:
+                half, c_run, row_tiles = runs[i - LAG]
+                mx_passes(acc[half], row_tiles, half, [c_run])
+                if half == 0 and c_run == PASSES - 1:
+                    for t in row_tiles:
+                        nc.vector.tensor_copy(out=pre_first[t][:], in_=acc[0][t][:])
+                        acc[1].append(sums.tile([P, H_HALF], F32, name="acc_second%d" % t, tag="acc"))
+            if i < len(slabs):
+                quantise(grouped, codes, scales)
+            if i < part1_slabs and i % 2 == 1:
+                t = i // 2 - (PASSES - B_TILES)
+                if t >= 0:
+                    nc.vector.tensor_tensor(out=result[t][:], in0=internal_sb[:, t, :], in1=mu_all[:], op=ALU.add)
+            if i >= part1_slabs:
+                t = i - part1_slabs - (LAG + 1)
+                if 0 <= t < B_TILES:
+                    nc.vector.bn_stats(out=stats[t][:, 0, :], in_=pre_first[t][:])
+        assert len(raw) == len(loads)
+        acc_second = acc[1]
+        for t in (2, 3):
+            mx_passes(acc_second, (t,), 1, range(PASSES))
+
+        for t in all_tiles:
+            nc.vector.bn_stats(out=stats[t][:, 1, :], in_=acc_second[t][:])
+            mean_var = keep.tile([P, 2], F32, name="mean_var%d" % t)
+            nc.vector.bn_aggr(out=mean_var[:], in_=stats[t][:].rearrange("p a s -> p (a s)"))
+            sd = keep.tile([P, 1], F32, name="sd%d" % t)
+            nc.scalar.activation(out=sd[:], in_=mean_var[:, 1:2], func=ACT.Sqrt)
+            nc.vector.tensor_scalar_add(out=sd[:], in0=sd[:], scalar1=EPS)
+            rstd = keep.tile([P, 1], F32, name="rstd%d" % t)
+            nc.vector.reciprocal(out=rstd[:], in_=sd[:])
+            shift = keep.tile([P, 1], F32, name="shift%d" % t)
+            nc.vector.tensor_scalar(
+                out=shift[:], in0=mean_var[:, 0:1], scalar1=rstd[:, 0:1], scalar2=-1.0, op0=ALU.mult, op1=ALU.mult
+            )
+            for cols, pre in ((first_cols, pre_first[t]), (second_cols, acc_second[t])):
+                nc.vector.scalar_tensor_tensor(
+                    out=result[t][:, cols],
+                    in0=pre[:],
+                    scalar=rstd[:, 0:1],
+                    in1=result[t][:, cols],
+                    op0=ALU.mult,
+                    op1=ALU.add,
+                )
+                nc.scalar.activation(
+                    out=result[t][:, cols], in_=result[t][:, cols], func=ACT.Relu, bias=shift[:, 0:1], scale=1.0
+                )
+                nc.sync.dma_start(out=out[t * P : (t + 1) * P, cols], in_=result[t][:, cols])

@@ -25,6 +25,8 @@ PASSES = K_TOTAL // K_PASS
 K_CHUNK = 2 * K_PASS
 RAW_BUFS = 8
 LAG = 3
+RUN = 2
+END_COLS = (slice(0, 256), slice(256, 512))
 EPS = 0.0001
 
 FLOPS = 2 * B * H * K_TOTAL
@@ -42,23 +44,20 @@ def tile_sparsegatedrnncell_pb_kernel(tc, x, hx, sy, internal, W_ih, W_hh, W_sh,
         ctx.enter_context(tc.manual_schedule())
 
         chunks = []
-        where_is = []
-        for act, weight in ((x, W_ih), (hx, W_hh), (sy, W_sh)):
-            for k0 in range(0, act.shape[1], K_CHUNK):
-                width = min(K_CHUNK, act.shape[1] - k0)
-                for local in range(width // K_PASS):
-                    where_is.append((len(chunks), local, width, local == width // K_PASS - 1))
-                chunks.append((act, weight, k0, width))
+        for act, weight, per_load in ((x, W_ih, 1), (hx, W_hh, 1), (sy, W_sh, 2)):
+            for k0 in range(0, act.shape[1], per_load * K_PASS):
+                chunks.append((act, weight, k0, per_load))
         loads = []
-        for n, (act, weight, k0, width) in enumerate(chunks):
-            loads.append((("act", n), act, 0, k0, width))
-            loads.append((("w", 0, n), weight, 0, k0, width))
-        for n, (act, weight, k0, width) in enumerate(chunks):
-            loads.append((("w", 1, n), weight, H_HALF, k0, width))
+        for n, (act, weight, k0, per_load) in enumerate(chunks):
+            loads.append((("act", n), act, 0, k0, per_load))
+            loads.append((("w", 0, n), weight, 0, k0, per_load))
+        for n, (act, weight, k0, per_load) in enumerate(chunks):
+            loads.append((("w", 1, n), weight, H_HALF, k0, per_load))
         raw = {}
 
         def issue_loads(count):
-            for key, source, row0, k0, width in loads[len(raw) : len(raw) + count]:
+            for key, source, row0, k0, per_load in loads[len(raw) : len(raw) + count]:
+                width = per_load * K_PASS
                 rows = raw_pool.tile([P, ROW_TILES * K_CHUNK], BF16, name="rows", tag="rows")
                 nc.sync.dma_start(
                     out=rows[:, 0 : ROW_TILES * width].rearrange("p (j k) -> p j k", j=ROW_TILES),
@@ -66,34 +65,24 @@ def tile_sparsegatedrnncell_pb_kernel(tc, x, hx, sy, internal, W_ih, W_hh, W_sh,
                 )
                 raw[key] = rows
 
-        mu_rows = const.tile([P, H], BF16)
-        nc.vector.memset(mu_rows[:], 0.0)
-        nc.sync.dma_start(out=mu_rows[0:1, :], in_=mu.rearrange("(o h) -> o h", o=1))
         issue_loads(RAW_BUFS)
+        mu_all = const.tile([P, H], BF16)
+        nc.sync.dma_start(out=mu_all[:], in_=mu.partition_broadcast(P))
         internal_sb = const.tile([P, B_TILES, H], BF16)
         nc.sync.dma_start(out=internal_sb[:], in_=internal.rearrange("(t p) h -> p t h", p=P))
 
-        ones = const.tile([P, P], BF16)
-        nc.vector.memset(ones[:], 1.0)
         warm = const.tile([P, 1], F32)
         nc.vector.memset(warm[:], 1.0)
         nc.scalar.activation(out=warm[:], in_=warm[:], func=ACT.Sqrt)
         ident = const.tile([P, P], F32)
         make_identity(nc, ident[:])
 
-        mu_all = const.tile([P, H], BF16)
-        for half in range(2):
-            cols = slice(half * H_HALF, (half + 1) * H_HALF)
-            spread = banks.tile([P, H_HALF], F32, tag="bank")
-            nc.tensor.matmul(out=spread[:], lhsT=ones[:], rhs=mu_rows[:, cols], start=True, stop=True)
-            nc.vector.tensor_copy(out=mu_all[:, cols], in_=spread[:])
-
         a_codes = keep.tile([P, PASSES, B], U32, align_bytes=64)
         a_scales = keep.tile([P, PASSES, B], U8, align_bytes=64)
         w_codes = keep.tile([P, PASSES, H], U32, align_bytes=64)
         w_scales = keep.tile([P, PASSES, H], U8, align_bytes=64)
 
-        def transpose_slab(rows, width, local):
+        def transpose_slab(rows, per_load, local):
             words = rows[:].bitcast(F32)
             grouped = stage.tile([P, SLAB_ROWS * PACK], BF16, align_bytes=64, tag="grouped")
             grouped_words = grouped[:].bitcast(F32).rearrange("p (j r u) -> p j r u", j=ROW_TILES, u=2)
@@ -101,7 +90,7 @@ def tile_sparsegatedrnncell_pb_kernel(tc, x, hx, sy, internal, W_ih, W_hh, W_sh,
                 bank = banks.tile([P, 2, 2, P], F32, tag="bank")
                 for j in range(2):
                     for u in range(2):
-                        first = (2 * pair + j) * (width // 2) + local * PASS_WORDS
+                        first = ((2 * pair + j) * per_load + local) * PASS_WORDS
                         nc.tensor.transpose(bank[:, j, u, :], words[:, first + u : first + PASS_WORDS : 2], ident[:])
                 nc.scalar.copy(
                     out=grouped_words[:, 2 * pair : 2 * pair + 2, :, :],
@@ -109,97 +98,105 @@ def tile_sparsegatedrnncell_pb_kernel(tc, x, hx, sy, internal, W_ih, W_hh, W_sh,
                 )
             return grouped
 
-        def quantise(grouped, codes, scales):
-            nc.vector.quantize_mx(out=codes.bitcast(FP8X4), scales=scales, in_=grouped[:])
+        def mx_pass(acc, t, half, c, cols=slice(0, H_HALF)):
+            b_cols = slice(t * P, (t + 1) * P)
+            h_cols = slice(half * H_HALF + cols.start, half * H_HALF + cols.stop)
+            nc.tensor.matmul_mx(
+                out=acc[:, cols],
+                lhsT=a_codes[:, c, b_cols].bitcast(FP8X4),
+                lhsT_scale=a_scales[:, c, b_cols],
+                rhs=w_codes[:, c, h_cols].bitcast(FP8X4),
+                rhs_scale=w_scales[:, c, h_cols],
+                start=(c == 0),
+                stop=(c == PASSES - 1),
+            )
 
-        def mx_passes(acc, row_tiles, half, pass_list):
-            h_cols = slice(half * H_HALF, (half + 1) * H_HALF)
-            for t in row_tiles:
-                b_cols = slice(t * P, (t + 1) * P)
-                for c in pass_list:
-                    nc.tensor.matmul_mx(
-                        out=acc[t][:],
-                        lhsT=a_codes[:, c, b_cols].bitcast(FP8X4),
-                        lhsT_scale=a_scales[:, c, b_cols],
-                        rhs=w_codes[:, c, h_cols].bitcast(FP8X4),
-                        rhs_scale=w_scales[:, c, h_cols],
-                        start=(c == 0),
-                        stop=(c == PASSES - 1),
-                    )
-
-        all_tiles = range(B_TILES)
         first_cols = slice(0, H_HALF)
         second_cols = slice(H_HALF, H)
         slabs = []
-        runs = []
-        for c in range(PASSES):
-            n = where_is[c][0]
-            slabs.append((("act", n), c, a_codes[:, c, :], a_scales[:, c, :]))
-            slabs.append((("w", 0, n), c, w_codes[:, c, first_cols], w_scales[:, c, first_cols]))
-            runs.append((0, c, (0, 1)))
-            runs.append((0, c, (2, 3)))
-        part1_slabs = len(slabs)
-        for c in range(PASSES):
-            n = where_is[c][0]
-            slabs.append((("w", 1, n), c, w_codes[:, c, second_cols], w_scales[:, c, second_cols]))
-            runs.append((1, c, (0, 1)))
+        ready = {}
+        first_pass = [sum(chunk[3] for chunk in chunks[:n]) for n in range(len(chunks))]
+        for key, source, row0, k0, per_load in loads:
+            for local in range(per_load):
+                c = first_pass[key[-1]] + local
+                if key[0] == "act":
+                    codes, scales = a_codes[:, c, :], a_scales[:, c, :]
+                else:
+                    cols = first_cols if key[1] == 0 else second_cols
+                    codes, scales = w_codes[:, c, cols], w_scales[:, c, cols]
+                    ready[(key[1], c)] = len(slabs)
+                slabs.append((key, per_load, local, local == per_load - 1, codes, scales))
+        part1_slabs = PASSES * 2
 
-        acc = {0: [sums.tile([P, H_HALF], F32, name="acc_first%d" % t, tag="acc") for t in all_tiles], 1: []}
-        result = [keep.tile([P, H], F32, name="result%d" % t) for t in all_tiles]
-        pre_first = [keep.tile([P, H_HALF], F32, name="pre_first%d" % t) for t in all_tiles]
-        stats = [keep.tile([P, 2, 6], F32, name="stats%d" % t) for t in all_tiles]
-        for i in range(len(slabs) + LAG):
-            if i < len(slabs):
-                key, c, codes, scales = slabs[i]
-                n, local, width, last_of_chunk = where_is[c]
-                grouped = transpose_slab(raw[key], width, local)
-                if last_of_chunk and len(raw) < len(loads):
-                    issue_loads(1)
-            if i >= LAG:
-                half, c_run, row_tiles = runs[i - LAG]
-                mx_passes(acc[half], row_tiles, half, [c_run])
-                if half == 0 and c_run == PASSES - 1:
-                    for t in row_tiles:
-                        nc.vector.tensor_copy(out=pre_first[t][:], in_=acc[0][t][:])
-                        acc[1].append(sums.tile([P, H_HALF], F32, name="acc_second%d" % t, tag="acc"))
-            if i < len(slabs):
-                quantise(grouped, codes, scales)
-            if i < part1_slabs and i % 2 == 1:
-                t = i // 2 - (PASSES - B_TILES)
-                if t >= 0:
-                    nc.vector.tensor_tensor(out=result[t][:], in0=internal_sb[:, t, :], in1=mu_all[:], op=ALU.add)
-            if i >= part1_slabs:
-                t = i - part1_slabs - (LAG + 1)
-                if 0 <= t < B_TILES:
-                    nc.vector.bn_stats(out=stats[t][:, 0, :], in_=pre_first[t][:])
-        assert len(raw) == len(loads)
-        acc_second = acc[1]
-        for t in (2, 3):
-            mx_passes(acc_second, (t,), 1, range(PASSES))
+        acc = {(0, t): sums.tile([P, H_HALF], F32, name="acc_first%d" % t, tag="acc") for t in range(B_TILES)}
+        todo = {0: [(c, t) for c in range(PASSES) for t in range(B_TILES)], 1: [(c, t) for t in range(B_TILES - 1) for c in range(PASSES)]}
+        result = [keep.tile([P, H], F32, name="result%d" % t) for t in range(B_TILES)]
+        pre_first = [keep.tile([P, H_HALF], F32, name="pre_first%d" % t) for t in range(B_TILES)]
+        stats = [keep.tile([P, 1 + len(END_COLS), 6], F32, name="stats%d" % t) for t in range(B_TILES)]
+        summed = []
 
-        for t in all_tiles:
-            nc.vector.bn_stats(out=stats[t][:, 1, :], in_=acc_second[t][:])
+        def run_passes(slab, count):
+            half = 0 if todo[0] else 1
+            possible = [(c, t) for c, t in todo[half] if ready[(half, c)] + LAG <= slab]
+            for c, t in possible[:count]:
+                todo[half].remove((c, t))
+                mx_pass(acc[(half, t)], t, half, c)
+                if half == 0 and c == PASSES - 1:
+                    nc.vector.tensor_copy(out=pre_first[t][:], in_=acc[(0, t)][:])
+                    acc[(1, t)] = sums.tile([P, H_HALF], F32, name="acc_second%d" % t, tag="acc")
+                    summed.append(t)
+
+        for i, (key, per_load, local, last_of_load, codes, scales) in enumerate(slabs):
+            grouped = transpose_slab(raw[key], per_load, local)
+            if last_of_load and len(raw) < len(loads):
+                issue_loads(1)
+            old_sums = list(summed)
+            run_passes(i, RUN)
+            nc.vector.quantize_mx(out=codes.bitcast(FP8X4), scales=scales, in_=grouped[:])
+            t = i // 2 - (PASSES - B_TILES)
+            if i < part1_slabs and i % 2 == 1 and t >= 0:
+                nc.vector.tensor_tensor(out=result[t][:], in0=internal_sb[:, t, :], in1=mu_all[:], op=ALU.add)
+            if old_sums:
+                t = summed.pop(0)
+                nc.vector.bn_stats(out=stats[t][:, 0, :], in_=pre_first[t][:])
+        assert len(raw) == len(loads) and not todo[0] and not summed
+
+        for t in range(B_TILES):
+            acc_t = acc[(1, t)]
+            if t < B_TILES - 1:
+                groups = (slice(0, H_HALF),)
+                run_passes(len(slabs) + LAG, len([1 for c, tile in todo[1] if tile == t]))
+            else:
+                groups = END_COLS
+                for cols in groups:
+                    for c in range(PASSES):
+                        mx_pass(acc_t, t, 1, c, cols)
+            for n, cols in enumerate(groups):
+                nc.vector.bn_stats(out=stats[t][:, 1 + n, :], in_=acc_t[:, cols])
             mean_var = keep.tile([P, 2], F32, name="mean_var%d" % t)
-            nc.vector.bn_aggr(out=mean_var[:], in_=stats[t][:].rearrange("p a s -> p (a s)"))
+            nc.vector.bn_aggr(out=mean_var[:], in_=stats[t][:, 0 : 1 + len(groups), :].rearrange("p a s -> p (a s)"))
             sd = keep.tile([P, 1], F32, name="sd%d" % t)
             nc.scalar.activation(out=sd[:], in_=mean_var[:, 1:2], func=ACT.Sqrt)
             nc.vector.tensor_scalar_add(out=sd[:], in0=sd[:], scalar1=EPS)
             rstd = keep.tile([P, 1], F32, name="rstd%d" % t)
             nc.vector.reciprocal(out=rstd[:], in_=sd[:])
             shift = keep.tile([P, 1], F32, name="shift%d" % t)
-            nc.vector.tensor_scalar(
-                out=shift[:], in0=mean_var[:, 0:1], scalar1=rstd[:, 0:1], scalar2=-1.0, op0=ALU.mult, op1=ALU.mult
-            )
-            for cols, pre in ((first_cols, pre_first[t]), (second_cols, acc_second[t])):
+            pieces = [(first_cols, pre_first[t][:])]
+            pieces += [(slice(H_HALF + cols.start, H_HALF + cols.stop), acc_t[:, cols]) for cols in groups]
+            for n, (cols, pre) in enumerate(pieces):
                 nc.vector.scalar_tensor_tensor(
                     out=result[t][:, cols],
-                    in0=pre[:],
-                    scalar=rstd[:, 0:1],
-                    in1=result[t][:, cols],
+                    in0=result[t][:, cols],
+                    scalar=sd[:, 0:1],
+                    in1=pre,
                     op0=ALU.mult,
                     op1=ALU.add,
                 )
+                if n == 0:
+                    nc.vector.tensor_scalar(
+                        out=shift[:], in0=mean_var[:, 0:1], scalar1=rstd[:, 0:1], scalar2=-1.0, op0=ALU.mult, op1=ALU.mult
+                    )
                 nc.scalar.activation(
-                    out=result[t][:, cols], in_=result[t][:, cols], func=ACT.Relu, bias=shift[:, 0:1], scale=1.0
+                    out=result[t][:, cols], in_=result[t][:, cols], func=ACT.Relu, bias=shift[:, 0:1], scale=rstd[:, 0:1]
                 )
                 nc.sync.dma_start(out=out[t * P : (t + 1) * P, cols], in_=result[t][:, cols])

@@ -25,7 +25,8 @@ PASSES = K_TOTAL // K_PASS
 K_CHUNK = 2 * K_PASS
 RAW_BUFS = 8
 LAG = 3
-RUN = 2
+RUN = 3
+FIRST_RUN = 10
 END_COLS = (slice(0, 256), slice(256, 512))
 EPS = 0.0001
 
@@ -66,8 +67,9 @@ def tile_sparsegatedrnncell_pb_kernel(tc, x, hx, sy, internal, W_ih, W_hh, W_sh,
                 raw[key] = rows
 
         issue_loads(RAW_BUFS)
-        mu_all = const.tile([P, H], BF16)
-        nc.sync.dma_start(out=mu_all[:], in_=mu.partition_broadcast(P))
+        mu_rows = const.tile([P, H], BF16)
+        nc.vector.memset(mu_rows[:], 0.0)
+        nc.sync.dma_start(out=mu_rows[0:1, :], in_=mu.rearrange("(o h) -> o h", o=1))
         internal_sb = const.tile([P, B_TILES, H], BF16)
         nc.sync.dma_start(out=internal_sb[:], in_=internal.rearrange("(t p) h -> p t h", p=P))
 
@@ -76,6 +78,14 @@ def tile_sparsegatedrnncell_pb_kernel(tc, x, hx, sy, internal, W_ih, W_hh, W_sh,
         nc.scalar.activation(out=warm[:], in_=warm[:], func=ACT.Sqrt)
         ident = const.tile([P, P], F32)
         make_identity(nc, ident[:])
+        ones = const.tile([P, P], BF16)
+        nc.vector.memset(ones[:], 1.0)
+        mu_all = const.tile([P, H], BF16)
+
+        def spread_mu(cols):
+            spread = banks.tile([P, H_HALF], F32, tag="bank")
+            nc.tensor.matmul(out=spread[:], lhsT=ones[:], rhs=mu_rows[:, cols], start=True, stop=True)
+            nc.vector.tensor_copy(out=mu_all[:, cols], in_=spread[:])
 
         a_codes = keep.tile([P, PASSES, B], U32, align_bytes=64)
         a_scales = keep.tile([P, PASSES, B], U8, align_bytes=64)
@@ -151,7 +161,11 @@ def tile_sparsegatedrnncell_pb_kernel(tc, x, hx, sy, internal, W_ih, W_hh, W_sh,
             if last_of_load and len(raw) < len(loads):
                 issue_loads(1)
             old_sums = list(summed)
-            run_passes(i, RUN)
+            if i == FIRST_RUN:
+                spread_mu(first_cols)
+                spread_mu(second_cols)
+            if i >= FIRST_RUN:
+                run_passes(i, RUN)
             nc.vector.quantize_mx(out=codes.bitcast(FP8X4), scales=scales, in_=grouped[:])
             t = i // 2 - (PASSES - B_TILES)
             if i < part1_slabs and i % 2 == 1 and t >= 0:

@@ -24,9 +24,9 @@ K_TOTAL = 512 + 1024 + 4096
 PASSES = K_TOTAL // K_PASS
 K_CHUNK = 2 * K_PASS
 RAW_BUFS = 8
-LAG = 3
-RUN = 3
-FIRST_RUN = 10
+LAG = 2
+RUN = 2
+WARM_UP = 5
 END_COLS = (slice(0, 256), slice(256, 512))
 EPS = 0.0001
 
@@ -66,6 +66,8 @@ def tile_sparsegatedrnncell_pb_kernel(tc, x, hx, sy, internal, W_ih, W_hh, W_sh,
                 )
                 raw[key] = rows
 
+        ones = const.tile([P, H_HALF], BF16)
+        nc.vector.memset(ones[:], 1.0)
         issue_loads(RAW_BUFS)
         mu_rows = const.tile([P, H], BF16)
         nc.vector.memset(mu_rows[:], 0.0)
@@ -78,13 +80,16 @@ def tile_sparsegatedrnncell_pb_kernel(tc, x, hx, sy, internal, W_ih, W_hh, W_sh,
         nc.scalar.activation(out=warm[:], in_=warm[:], func=ACT.Sqrt)
         ident = const.tile([P, P], F32)
         make_identity(nc, ident[:])
-        ones = const.tile([P, P], BF16)
-        nc.vector.memset(ones[:], 1.0)
         mu_all = const.tile([P, H], BF16)
+
+        def keep_busy(count):
+            unread = banks.tile([P, H_HALF], F32, tag="bank")
+            for n in range(count):
+                nc.tensor.matmul(out=unread[:], lhsT=ones[:, 0:P], rhs=ones[:], start=True, stop=True)
 
         def spread_mu(cols):
             spread = banks.tile([P, H_HALF], F32, tag="bank")
-            nc.tensor.matmul(out=spread[:], lhsT=ones[:], rhs=mu_rows[:, cols], start=True, stop=True)
+            nc.tensor.matmul(out=spread[:], lhsT=ones[:, 0:P], rhs=mu_rows[:, cols], start=True, stop=True)
             nc.vector.tensor_copy(out=mu_all[:, cols], in_=spread[:])
 
         a_codes = keep.tile([P, PASSES, B], U32, align_bytes=64)
@@ -126,16 +131,16 @@ def tile_sparsegatedrnncell_pb_kernel(tc, x, hx, sy, internal, W_ih, W_hh, W_sh,
         slabs = []
         ready = {}
         first_pass = [sum(chunk[3] for chunk in chunks[:n]) for n in range(len(chunks))]
-        for key, source, row0, k0, per_load in loads:
-            for local in range(per_load):
-                c = first_pass[key[-1]] + local
-                if key[0] == "act":
-                    codes, scales = a_codes[:, c, :], a_scales[:, c, :]
-                else:
-                    cols = first_cols if key[1] == 0 else second_cols
-                    codes, scales = w_codes[:, c, cols], w_scales[:, c, cols]
-                    ready[(key[1], c)] = len(slabs)
-                slabs.append((key, per_load, local, local == per_load - 1, codes, scales))
+        for part in range(2):
+            for n, (act, weight, k0, per_load) in enumerate(chunks):
+                for local in range(per_load):
+                    c = first_pass[n] + local
+                    last_of_load = local == per_load - 1
+                    if part == 0:
+                        slabs.append((("act", n), per_load, local, last_of_load, a_codes[:, c, :], a_scales[:, c, :]))
+                    cols = (first_cols, second_cols)[part]
+                    ready[(part, c)] = len(slabs)
+                    slabs.append((("w", part, n), per_load, local, last_of_load, w_codes[:, c, cols], w_scales[:, c, cols]))
         part1_slabs = PASSES * 2
 
         acc = {(0, t): sums.tile([P, H_HALF], F32, name="acc_first%d" % t, tag="acc") for t in range(B_TILES)}
@@ -156,16 +161,18 @@ def tile_sparsegatedrnncell_pb_kernel(tc, x, hx, sy, internal, W_ih, W_hh, W_sh,
                     acc[(1, t)] = sums.tile([P, H_HALF], F32, name="acc_second%d" % t, tag="acc")
                     summed.append(t)
 
+        keep_busy(WARM_UP)
         for i, (key, per_load, local, last_of_load, codes, scales) in enumerate(slabs):
             grouped = transpose_slab(raw[key], per_load, local)
             if last_of_load and len(raw) < len(loads):
                 issue_loads(1)
             old_sums = list(summed)
-            if i == FIRST_RUN:
+            if i < LAG:
+                keep_busy(RUN)
+            elif i == LAG:
                 spread_mu(first_cols)
                 spread_mu(second_cols)
-            if i >= FIRST_RUN:
-                run_passes(i, RUN)
+            run_passes(i, RUN)
             nc.vector.quantize_mx(out=codes.bitcast(FP8X4), scales=scales, in_=grouped[:])
             t = i // 2 - (PASSES - B_TILES)
             if i < part1_slabs and i % 2 == 1 and t >= 0:

@@ -23,10 +23,11 @@ ROW_TILES = SLAB_ROWS // P
 K_TOTAL = 512 + 1024 + 4096
 PASSES = K_TOTAL // K_PASS
 K_CHUNK = 2 * K_PASS
-RAW_BUFS = 8
-LAG = 2
+RAW_BUFS = 10
+LAG = 3
 RUN = 2
 WARM_UP = 5
+MU_SLAB = 12
 END_COLS = (slice(0, 256), slice(256, 512))
 EPS = 0.0001
 
@@ -68,9 +69,9 @@ def tile_sparsegatedrnncell_pb_kernel(tc, x, hx, sy, internal, W_ih, W_hh, W_sh,
 
         ones = const.tile([P, H_HALF], BF16)
         nc.vector.memset(ones[:], 1.0)
-        issue_loads(RAW_BUFS)
         mu_rows = const.tile([P, H], BF16)
         nc.vector.memset(mu_rows[:], 0.0)
+        issue_loads(RAW_BUFS)
         nc.sync.dma_start(out=mu_rows[0:1, :], in_=mu.rearrange("(o h) -> o h", o=1))
         internal_sb = const.tile([P, B_TILES, H], BF16)
         nc.sync.dma_start(out=internal_sb[:], in_=internal.rearrange("(t p) h -> p t h", p=P))
@@ -167,9 +168,9 @@ def tile_sparsegatedrnncell_pb_kernel(tc, x, hx, sy, internal, W_ih, W_hh, W_sh,
             if last_of_load and len(raw) < len(loads):
                 issue_loads(1)
             old_sums = list(summed)
-            if i < LAG:
+            if i <= LAG:
                 keep_busy(RUN)
-            elif i == LAG:
+            if i == MU_SLAB:
                 spread_mu(first_cols)
                 spread_mu(second_cols)
             run_passes(i, RUN)

@@ -23,12 +23,14 @@ ROW_TILES = SLAB_ROWS // P
 K_TOTAL = 512 + 1024 + 4096
 PASSES = K_TOTAL // K_PASS
 K_CHUNK = 2 * K_PASS
-RAW_BUFS = 10
+RAW_BUFS = 8
 LAG = 3
 RUN = 2
 WARM_UP = 5
 MU_SLAB = 12
 END_COLS = (slice(0, 256), slice(256, 512))
+SORTED_PASSES = (4, 6, 8, 10)
+SORT_AHEAD = 2
 EPS = 0.0001
 
 FLOPS = 2 * B * H * K_TOTAL
@@ -41,6 +43,7 @@ def tile_sparsegatedrnncell_pb_kernel(tc, x, hx, sy, internal, W_ih, W_hh, W_sh,
         keep = ctx.enter_context(tc.tile_pool(name="keep", bufs=1))
         raw_pool = ctx.enter_context(tc.tile_pool(name="raw_pool", bufs=RAW_BUFS))
         stage = ctx.enter_context(tc.tile_pool(name="stage", bufs=4))
+        sorted_pool = ctx.enter_context(tc.tile_pool(name="sorted_pool", bufs=SORT_AHEAD + 1))
         banks = ctx.enter_context(tc.psum_pool(name="banks", bufs=4))
         sums = ctx.enter_context(tc.psum_pool(name="sums", bufs=4))
         ctx.enter_context(tc.manual_schedule())
@@ -98,16 +101,31 @@ def tile_sparsegatedrnncell_pb_kernel(tc, x, hx, sy, internal, W_ih, W_hh, W_sh,
         w_codes = keep.tile([P, PASSES, H], U32, align_bytes=64)
         w_scales = keep.tile([P, PASSES, H], U8, align_bytes=64)
 
-        def transpose_slab(rows, per_load, local):
-            words = rows[:].bitcast(F32)
+        def sort_slab(rows, per_load, local):
+            ordered = sorted_pool.tile([P, ROW_TILES * K_PASS], BF16, align_bytes=64, tag="ordered")
+            loaded = rows[:, 0 : ROW_TILES * per_load * K_PASS].rearrange("p (j l k) -> p j l k", j=ROW_TILES, l=per_load)
+            nc.vector.tensor_copy(
+                out=ordered[:].rearrange("p (u j q e) -> p j q u e", u=2, j=ROW_TILES, e=16),
+                in_=loaded[:, :, local, :].rearrange("p j (q u e) -> p j q u e", u=2, e=16),
+            )
+            return ordered
+
+        def transpose_slab(rows, per_load, local, ordered):
+            words = (rows if ordered is None else ordered)[:].bitcast(F32)
             grouped = stage.tile([P, SLAB_ROWS * PACK], BF16, align_bytes=64, tag="grouped")
             grouped_words = grouped[:].bitcast(F32).rearrange("p (j r u) -> p j r u", j=ROW_TILES, u=2)
             for pair in range(ROW_TILES // 2):
                 bank = banks.tile([P, 2, 2, P], F32, tag="bank")
                 for j in range(2):
                     for u in range(2):
-                        first = ((2 * pair + j) * per_load + local) * PASS_WORDS
-                        nc.tensor.transpose(bank[:, j, u, :], words[:, first + u : first + PASS_WORDS : 2], ident[:])
+                        row_tile = 2 * pair + j
+                        if ordered is None:
+                            first = (row_tile * per_load + local) * PASS_WORDS
+                            these = words[:, first + u : first + PASS_WORDS : 2]
+                        else:
+                            first = (u * ROW_TILES + row_tile) * P
+                            these = words[:, first : first + P]
+                        nc.tensor.transpose(bank[:, j, u, :], these, ident[:])
                 nc.scalar.copy(
                     out=grouped_words[:, 2 * pair : 2 * pair + 2, :, :],
                     in_=bank[:].rearrange("p j u r -> p j r u"),
@@ -163,8 +181,14 @@ def tile_sparsegatedrnncell_pb_kernel(tc, x, hx, sy, internal, W_ih, W_hh, W_sh,
                     summed.append(t)
 
         keep_busy(WARM_UP)
+        ordered = {}
         for i, (key, per_load, local, last_of_load, codes, scales) in enumerate(slabs):
-            grouped = transpose_slab(raw[key], per_load, local)
+            ahead = i + SORT_AHEAD
+            if ahead < len(slabs):
+                soon, soon_passes, soon_local = slabs[ahead][0:3]
+                if first_pass[soon[-1]] + soon_local in SORTED_PASSES:
+                    ordered[ahead] = sort_slab(raw[soon], soon_passes, soon_local)
+            grouped = transpose_slab(raw[key], per_load, local, ordered.get(i))
             if last_of_load and len(raw) < len(loads):
                 issue_loads(1)
             old_sums = list(summed)
@@ -187,14 +211,16 @@ def tile_sparsegatedrnncell_pb_kernel(tc, x, hx, sy, internal, W_ih, W_hh, W_sh,
             acc_t = acc[(1, t)]
             if t < B_TILES - 1:
                 groups = (slice(0, H_HALF),)
+                acc_t = [acc_t]
                 run_passes(len(slabs) + LAG, len([1 for c, tile in todo[1] if tile == t]))
             else:
                 groups = END_COLS
-                for cols in groups:
+                acc_t = [acc_t] + [banks.tile([P, H_HALF], F32, name="acc_end", tag="bank") for cols in groups[1:]]
+                for bank, cols in zip(acc_t, groups):
                     for c in range(PASSES):
-                        mx_pass(acc_t, t, 1, c, cols)
+                        mx_pass(bank, t, 1, c, cols)
             for n, cols in enumerate(groups):
-                nc.vector.bn_stats(out=stats[t][:, 1 + n, :], in_=acc_t[:, cols])
+                nc.vector.bn_stats(out=stats[t][:, 1 + n, :], in_=acc_t[n][:, cols])
             mean_var = keep.tile([P, 2], F32, name="mean_var%d" % t)
             nc.vector.bn_aggr(out=mean_var[:], in_=stats[t][:, 0 : 1 + len(groups), :].rearrange("p a s -> p (a s)"))
             sd = keep.tile([P, 1], F32, name="sd%d" % t)
@@ -204,7 +230,7 @@ def tile_sparsegatedrnncell_pb_kernel(tc, x, hx, sy, internal, W_ih, W_hh, W_sh,
             nc.vector.reciprocal(out=rstd[:], in_=sd[:])
             shift = keep.tile([P, 1], F32, name="shift%d" % t)
             pieces = [(first_cols, pre_first[t][:])]
-            pieces += [(slice(H_HALF + cols.start, H_HALF + cols.stop), acc_t[:, cols]) for cols in groups]
+            pieces += [(slice(H_HALF + cols.start, H_HALF + cols.stop), bank[:, cols]) for bank, cols in zip(acc_t, groups)]
             for n, (cols, pre) in enumerate(pieces):
                 nc.vector.scalar_tensor_tensor(
                     out=result[t][:, cols],

@@ -23,13 +23,15 @@ ROW_TILES = SLAB_ROWS // P
 K_TOTAL = 512 + 1024 + 4096
 PASSES = K_TOTAL // K_PASS
 K_CHUNK = 2 * K_PASS
+ACTS = "acts"
+CUTS = (((1,), (2,), (2, 2, 2, 2)), ((1,), (2,), (2, 2, 2, 2)))
 RAW_BUFS = 8
 LAG = 3
 RUN = 2
 WARM_UP = 5
 MU_SLAB = 12
 END_COLS = (slice(0, 256), slice(256, 512))
-SORTED_PASSES = (4, 6, 8, 10)
+SORTED_PASSES = (8, 10)
 SORT_AHEAD = 2
 EPS = 0.0001
 
@@ -42,33 +44,38 @@ def tile_sparsegatedrnncell_pb_kernel(tc, x, hx, sy, internal, W_ih, W_hh, W_sh,
         const = ctx.enter_context(tc.tile_pool(name="const", bufs=1))
         keep = ctx.enter_context(tc.tile_pool(name="keep", bufs=1))
         raw_pool = ctx.enter_context(tc.tile_pool(name="raw_pool", bufs=RAW_BUFS))
+        long_pool = ctx.enter_context(tc.tile_pool(name="long_pool", bufs=2))
         stage = ctx.enter_context(tc.tile_pool(name="stage", bufs=4))
         sorted_pool = ctx.enter_context(tc.tile_pool(name="sorted_pool", bufs=SORT_AHEAD + 1))
         banks = ctx.enter_context(tc.psum_pool(name="banks", bufs=4))
         sums = ctx.enter_context(tc.psum_pool(name="sums", bufs=4))
         ctx.enter_context(tc.manual_schedule())
 
-        chunks = []
-        for act, weight, per_load in ((x, W_ih, 1), (hx, W_hh, 1), (sy, W_sh, 2)):
-            for k0 in range(0, act.shape[1], per_load * K_PASS):
-                chunks.append((act, weight, k0, per_load))
         loads = []
-        for n, (act, weight, k0, per_load) in enumerate(chunks):
-            loads.append((("act", n), act, 0, k0, per_load))
-            loads.append((("w", 0, n), weight, 0, k0, per_load))
-        for n, (act, weight, k0, per_load) in enumerate(chunks):
-            loads.append((("w", 1, n), weight, H_HALF, k0, per_load))
+        for part, cuts in enumerate(CUTS):
+            first = 0
+            for (act, weight), stream_cuts in zip(((x, W_ih), (hx, W_hh), (sy, W_sh)), cuts):
+                k0 = 0
+                for passes in stream_cuts:
+                    if part == 0:
+                        loads.append((ACTS, first, passes, act, 0, k0))
+                    loads.append((part, first, passes, weight, part * H_HALF, k0))
+                    first += passes
+                    k0 += passes * K_PASS
         raw = {}
 
         def issue_loads(count):
-            for key, source, row0, k0, per_load in loads[len(raw) : len(raw) + count]:
+            for what, first, per_load, source, row0, k0 in loads[len(raw) : len(raw) + count]:
                 width = per_load * K_PASS
-                rows = raw_pool.tile([P, ROW_TILES * K_CHUNK], BF16, name="rows", tag="rows")
+                if per_load > 2:
+                    rows = long_pool.tile([P, ROW_TILES * width], BF16, name="long_rows", tag="long_rows")
+                else:
+                    rows = raw_pool.tile([P, ROW_TILES * K_CHUNK], BF16, name="rows", tag="rows")
                 nc.sync.dma_start(
                     out=rows[:, 0 : ROW_TILES * width].rearrange("p (j k) -> p j k", j=ROW_TILES),
-                    in_=source[row0 : row0 + SLAB_ROWS, k0 : k0 + width].rearrange("(j p) k -> p j k", p=P),
+                    in_=source[row0 : row0 + SLAB_ROWS, k0 : k0 + width].rearrange("(p j) k -> p j k", j=ROW_TILES),
                 )
-                raw[key] = rows
+                raw[(what, first)] = rows
 
         ones = const.tile([P, H_HALF], BF16)
         nc.vector.memset(ones[:], 1.0)
@@ -77,7 +84,7 @@ def tile_sparsegatedrnncell_pb_kernel(tc, x, hx, sy, internal, W_ih, W_hh, W_sh,
         issue_loads(RAW_BUFS)
         nc.sync.dma_start(out=mu_rows[0:1, :], in_=mu.rearrange("(o h) -> o h", o=1))
         internal_sb = const.tile([P, B_TILES, H], BF16)
-        nc.sync.dma_start(out=internal_sb[:], in_=internal.rearrange("(t p) h -> p t h", p=P))
+        nc.sync.dma_start(out=internal_sb[:], in_=internal.rearrange("(p t) h -> p t h", t=B_TILES))
 
         warm = const.tile([P, 1], F32)
         nc.vector.memset(warm[:], 1.0)
@@ -110,10 +117,10 @@ def tile_sparsegatedrnncell_pb_kernel(tc, x, hx, sy, internal, W_ih, W_hh, W_sh,
             )
             return ordered
 
-        def transpose_slab(rows, per_load, local, ordered):
+        def transpose_slab(rows, per_load, local, ordered, in_row_order):
             words = (rows if ordered is None else ordered)[:].bitcast(F32)
             grouped = stage.tile([P, SLAB_ROWS * PACK], BF16, align_bytes=64, tag="grouped")
-            grouped_words = grouped[:].bitcast(F32).rearrange("p (j r u) -> p j r u", j=ROW_TILES, u=2)
+            words_out = grouped[:].bitcast(F32)
             for pair in range(ROW_TILES // 2):
                 bank = banks.tile([P, 2, 2, P], F32, tag="bank")
                 for j in range(2):
@@ -126,10 +133,17 @@ def tile_sparsegatedrnncell_pb_kernel(tc, x, hx, sy, internal, W_ih, W_hh, W_sh,
                             first = (u * ROW_TILES + row_tile) * P
                             these = words[:, first : first + P]
                         nc.tensor.transpose(bank[:, j, u, :], these, ident[:])
-                nc.scalar.copy(
-                    out=grouped_words[:, 2 * pair : 2 * pair + 2, :, :],
-                    in_=bank[:].rearrange("p j u r -> p j r u"),
-                )
+                two = slice(2 * pair, 2 * pair + 2)
+                if in_row_order:
+                    nc.scalar.copy(
+                        out=words_out.rearrange("p (r j u) -> p r j u", j=ROW_TILES, u=2)[:, :, two, :],
+                        in_=bank[:].rearrange("p j u r -> p r j u"),
+                    )
+                else:
+                    nc.scalar.copy(
+                        out=words_out.rearrange("p (j r u) -> p j r u", j=ROW_TILES, u=2)[:, two, :, :],
+                        in_=bank[:].rearrange("p j u r -> p j r u"),
+                    )
             return grouped
 
         def mx_pass(acc, t, half, c, cols=slice(0, H_HALF)):
@@ -149,17 +163,25 @@ def tile_sparsegatedrnncell_pb_kernel(tc, x, hx, sy, internal, W_ih, W_hh, W_sh,
         second_cols = slice(H_HALF, H)
         slabs = []
         ready = {}
-        first_pass = [sum(chunk[3] for chunk in chunks[:n]) for n in range(len(chunks))]
-        for part in range(2):
-            for n, (act, weight, k0, per_load) in enumerate(chunks):
-                for local in range(per_load):
-                    c = first_pass[n] + local
-                    last_of_load = local == per_load - 1
-                    if part == 0:
-                        slabs.append((("act", n), per_load, local, last_of_load, a_codes[:, c, :], a_scales[:, c, :]))
-                    cols = (first_cols, second_cols)[part]
-                    ready[(part, c)] = len(slabs)
-                    slabs.append((("w", part, n), per_load, local, last_of_load, w_codes[:, c, cols], w_scales[:, c, cols]))
+        held = []
+        for what, first, passes, source, row0, k0 in loads:
+            held.append([(what, first, passes, local) for local in range(passes)])
+            if what == ACTS:
+                continue
+            if len(held) == 2 and source is W_sh:
+                order = [which[local] for local in range(passes) for which in held]
+            else:
+                order = [slab for which in held for slab in which]
+            held = []
+            for which, start, count, local in order:
+                c = start + local
+                if which == ACTS:
+                    codes, scales = a_codes[:, c, :], a_scales[:, c, :]
+                else:
+                    cols = (first_cols, second_cols)[which]
+                    codes, scales = w_codes[:, c, cols], w_scales[:, c, cols]
+                    ready[(which, c)] = len(slabs)
+                slabs.append(((which, start), count, local, local == count - 1, c, codes, scales))
         part1_slabs = PASSES * 2
 
         acc = {(0, t): sums.tile([P, H_HALF], F32, name="acc_first%d" % t, tag="acc") for t in range(B_TILES)}
@@ -179,25 +201,25 @@ def tile_sparsegatedrnncell_pb_kernel(tc, x, hx, sy, internal, W_ih, W_hh, W_sh,
                     nc.vector.tensor_copy(out=pre_first[t][:], in_=acc[(0, t)][:])
                     acc[(1, t)] = sums.tile([P, H_HALF], F32, name="acc_second%d" % t, tag="acc")
                     summed.append(t)
+            return len(possible[:count])
 
         keep_busy(WARM_UP)
         ordered = {}
-        for i, (key, per_load, local, last_of_load, codes, scales) in enumerate(slabs):
+        for i, (key, per_load, local, last_of_load, c_slab, codes, scales) in enumerate(slabs):
             ahead = i + SORT_AHEAD
             if ahead < len(slabs):
-                soon, soon_passes, soon_local = slabs[ahead][0:3]
-                if first_pass[soon[-1]] + soon_local in SORTED_PASSES:
+                soon, soon_passes, soon_local, last, soon_pass = slabs[ahead][0:5]
+                if soon_pass in SORTED_PASSES:
                     ordered[ahead] = sort_slab(raw[soon], soon_passes, soon_local)
-            grouped = transpose_slab(raw[key], per_load, local, ordered.get(i))
+            grouped = transpose_slab(raw[key], per_load, local, ordered.get(i), key[0] != ACTS)
             if last_of_load and len(raw) < len(loads):
                 issue_loads(1)
             old_sums = list(summed)
-            if i <= LAG:
-                keep_busy(RUN)
             if i == MU_SLAB:
                 spread_mu(first_cols)
                 spread_mu(second_cols)
-            run_passes(i, RUN)
+            if run_passes(i, RUN) == 0:
+                keep_busy(RUN)
             nc.vector.quantize_mx(out=codes.bitcast(FP8X4), scales=scales, in_=grouped[:])
             t = i // 2 - (PASSES - B_TILES)
             if i < part1_slabs and i % 2 == 1 and t >= 0:
@@ -247,4 +269,4 @@ def tile_sparsegatedrnncell_pb_kernel(tc, x, hx, sy, internal, W_ih, W_hh, W_sh,
                 nc.scalar.activation(
                     out=result[t][:, cols], in_=result[t][:, cols], func=ACT.Relu, bias=shift[:, 0:1], scale=rstd[:, 0:1]
                 )
-                nc.sync.dma_start(out=out[t * P : (t + 1) * P, cols], in_=result[t][:, cols])
+                nc.sync.dma_start(out=out.rearrange("(p t) h -> p t h", t=B_TILES)[:, t, cols], in_=result[t][:, cols])

@@ -24,15 +24,15 @@ K_TOTAL = 512 + 1024 + 4096
 PASSES = K_TOTAL // K_PASS
 K_CHUNK = 2 * K_PASS
 ACTS = "acts"
-CUTS = (((1,), (2,), (2, 2, 2, 2)), ((1,), (2,), (2, 2, 2, 2)))
+CUTS = (((1,), (2,), (2, 2, 2, 2)), ((1,), (2,), (4, 2, 2)))
 RAW_BUFS = 8
 LAG = 3
 RUN = 2
 WARM_UP = 5
-MU_SLAB = 12
+MU_SLAB = 3
 END_COLS = (slice(0, 256), slice(256, 512))
-SORTED_PASSES = (8, 10)
-SORT_AHEAD = 2
+SORTED_PASSES = (4, 6, 8, 10)
+SORT_AHEAD = 3
 EPS = 0.0001
 
 FLOPS = 2 * B * H * K_TOTAL
@@ -44,8 +44,8 @@ def tile_sparsegatedrnncell_pb_kernel(tc, x, hx, sy, internal, W_ih, W_hh, W_sh,
         const = ctx.enter_context(tc.tile_pool(name="const", bufs=1))
         keep = ctx.enter_context(tc.tile_pool(name="keep", bufs=1))
         raw_pool = ctx.enter_context(tc.tile_pool(name="raw_pool", bufs=RAW_BUFS))
-        long_pool = ctx.enter_context(tc.tile_pool(name="long_pool", bufs=2))
-        stage = ctx.enter_context(tc.tile_pool(name="stage", bufs=4))
+        long_pool = ctx.enter_context(tc.tile_pool(name="long_pool", bufs=1))
+        stage = ctx.enter_context(tc.tile_pool(name="stage", bufs=3))
         sorted_pool = ctx.enter_context(tc.tile_pool(name="sorted_pool", bufs=SORT_AHEAD + 1))
         banks = ctx.enter_context(tc.psum_pool(name="banks", bufs=4))
         sums = ctx.enter_context(tc.psum_pool(name="sums", bufs=4))
@@ -81,8 +81,9 @@ def tile_sparsegatedrnncell_pb_kernel(tc, x, hx, sy, internal, W_ih, W_hh, W_sh,
         nc.vector.memset(ones[:], 1.0)
         mu_rows = const.tile([P, H], BF16)
         nc.vector.memset(mu_rows[:], 0.0)
-        issue_loads(RAW_BUFS)
+        issue_loads(2)
         nc.sync.dma_start(out=mu_rows[0:1, :], in_=mu.rearrange("(o h) -> o h", o=1))
+        issue_loads(RAW_BUFS - 2)
         internal_sb = const.tile([P, B_TILES, H], BF16)
         nc.sync.dma_start(out=internal_sb[:], in_=internal.rearrange("(p t) h -> p t h", t=B_TILES))
 
@@ -218,7 +219,7 @@ def tile_sparsegatedrnncell_pb_kernel(tc, x, hx, sy, internal, W_ih, W_hh, W_sh,
             if i == MU_SLAB:
                 spread_mu(first_cols)
                 spread_mu(second_cols)
-            if run_passes(i, RUN) == 0:
+            elif run_passes(i, RUN) == 0:
                 keep_busy(RUN)
             nc.vector.quantize_mx(out=codes.bitcast(FP8X4), scales=scales, in_=grouped[:])
             t = i // 2 - (PASSES - B_TILES)

@@ -27,12 +27,15 @@ ACTS = "acts"
 CUTS = (((1,), (2,), (2, 2, 2, 2)), ((1,), (2,), (4, 2, 2)))
 RAW_BUFS = 8
 LAG = 3
+EARLY_LAG = 2
 RUN = 2
 WARM_UP = 5
 MU_SLAB = 3
 END_COLS = (slice(0, 256), slice(256, 512))
 SORTED_PASSES = (4, 6, 8, 10)
 SORT_AHEAD = 3
+INTERNAL_AFTER = 11
+DRIVE_SLABS = (15, 17, 19, 21)
 EPS = 0.0001
 
 FLOPS = 2 * B * H * K_TOTAL
@@ -63,6 +66,7 @@ def tile_sparsegatedrnncell_pb_kernel(tc, x, hx, sy, internal, W_ih, W_hh, W_sh,
                     first += passes
                     k0 += passes * K_PASS
         raw = {}
+        internal_sb = const.tile([P, B_TILES, H], BF16)
 
         def issue_loads(count):
             for what, first, per_load, source, row0, k0 in loads[len(raw) : len(raw) + count]:
@@ -76,6 +80,8 @@ def tile_sparsegatedrnncell_pb_kernel(tc, x, hx, sy, internal, W_ih, W_hh, W_sh,
                     in_=source[row0 : row0 + SLAB_ROWS, k0 : k0 + width].rearrange("(p j) k -> p j k", j=ROW_TILES),
                 )
                 raw[(what, first)] = rows
+                if len(raw) == INTERNAL_AFTER:
+                    nc.sync.dma_start(out=internal_sb[:], in_=internal.rearrange("(p t) h -> p t h", t=B_TILES))
 
         ones = const.tile([P, H_HALF], BF16)
         nc.vector.memset(ones[:], 1.0)
@@ -84,8 +90,6 @@ def tile_sparsegatedrnncell_pb_kernel(tc, x, hx, sy, internal, W_ih, W_hh, W_sh,
         issue_loads(2)
         nc.sync.dma_start(out=mu_rows[0:1, :], in_=mu.rearrange("(o h) -> o h", o=1))
         issue_loads(RAW_BUFS - 2)
-        internal_sb = const.tile([P, B_TILES, H], BF16)
-        nc.sync.dma_start(out=internal_sb[:], in_=internal.rearrange("(p t) h -> p t h", t=B_TILES))
 
         warm = const.tile([P, 1], F32)
         nc.vector.memset(warm[:], 1.0)
@@ -194,7 +198,7 @@ def tile_sparsegatedrnncell_pb_kernel(tc, x, hx, sy, internal, W_ih, W_hh, W_sh,
 
         def run_passes(slab, count):
             half = 0 if todo[0] else 1
-            possible = [(c, t) for c, t in todo[half] if ready[(half, c)] + LAG <= slab]
+            possible = [(c, t) for c, t in todo[half] if ready[(half, c)] + (LAG if slab > 6 else EARLY_LAG) <= slab]
             for c, t in possible[:count]:
                 todo[half].remove((c, t))
                 mx_pass(acc[(half, t)], t, half, c)
@@ -222,52 +226,70 @@ def tile_sparsegatedrnncell_pb_kernel(tc, x, hx, sy, internal, W_ih, W_hh, W_sh,
             elif run_passes(i, RUN) == 0:
                 keep_busy(RUN)
             nc.vector.quantize_mx(out=codes.bitcast(FP8X4), scales=scales, in_=grouped[:])
-            t = i // 2 - (PASSES - B_TILES)
-            if i < part1_slabs and i % 2 == 1 and t >= 0:
+            if i in DRIVE_SLABS:
+                t = DRIVE_SLABS.index(i)
                 nc.vector.tensor_tensor(out=result[t][:], in0=internal_sb[:, t, :], in1=mu_all[:], op=ALU.add)
             if old_sums:
                 t = summed.pop(0)
                 nc.vector.bn_stats(out=stats[t][:, 0, :], in_=pre_first[t][:])
         assert len(raw) == len(loads) and not todo[0] and not summed
 
-        for t in range(B_TILES):
-            acc_t = acc[(1, t)]
-            if t < B_TILES - 1:
-                groups = (slice(0, H_HALF),)
-                acc_t = [acc_t]
-                run_passes(len(slabs) + LAG, len([1 for c, tile in todo[1] if tile == t]))
-            else:
-                groups = END_COLS
-                acc_t = [acc_t] + [banks.tile([P, H_HALF], F32, name="acc_end", tag="bank") for cols in groups[1:]]
-                for bank, cols in zip(acc_t, groups):
-                    for c in range(PASSES):
-                        mx_pass(bank, t, 1, c, cols)
-            for n, cols in enumerate(groups):
-                nc.vector.bn_stats(out=stats[t][:, 1 + n, :], in_=acc_t[n][:, cols])
-            mean_var = keep.tile([P, 2], F32, name="mean_var%d" % t)
-            nc.vector.bn_aggr(out=mean_var[:], in_=stats[t][:, 0 : 1 + len(groups), :].rearrange("p a s -> p (a s)"))
-            sd = keep.tile([P, 1], F32, name="sd%d" % t)
-            nc.scalar.activation(out=sd[:], in_=mean_var[:, 1:2], func=ACT.Sqrt)
-            nc.vector.tensor_scalar_add(out=sd[:], in0=sd[:], scalar1=EPS)
-            rstd = keep.tile([P, 1], F32, name="rstd%d" % t)
-            nc.vector.reciprocal(out=rstd[:], in_=sd[:])
-            shift = keep.tile([P, 1], F32, name="shift%d" % t)
-            pieces = [(first_cols, pre_first[t][:])]
-            pieces += [(slice(H_HALF + cols.start, H_HALF + cols.stop), bank[:, cols]) for bank, cols in zip(acc_t, groups)]
-            for n, (cols, pre) in enumerate(pieces):
+        for i in range(len(slabs), len(slabs) + LAG):
+            run_passes(i, RUN)
+        last = B_TILES - 1
+        for t in range(last):
+            run_passes(len(slabs) + LAG, PASSES)
+        banks_of = {t: [acc[(1, t)]] for t in range(B_TILES)}
+        banks_of[last] += [banks.tile([P, H_HALF], F32, name="acc_end", tag="bank") for cols in END_COLS[1:]]
+        groups_of = {t: (slice(0, H_HALF),) for t in range(last)}
+        groups_of[last] = END_COLS
+        for bank, cols in zip(banks_of[last], END_COLS):
+            for c in range(PASSES):
+                mx_pass(bank, last, 1, c, cols)
+
+        mean_var = [keep.tile([P, 2], F32, name="mean_var%d" % t) for t in range(B_TILES)]
+        sd = [keep.tile([P, 1], F32, name="sd%d" % t) for t in range(B_TILES)]
+        rstd = [keep.tile([P, 1], F32, name="rstd%d" % t) for t in range(B_TILES)]
+        shift = [keep.tile([P, 1], F32, name="shift%d" % t) for t in range(B_TILES)]
+
+        def statistics(t):
+            for n, cols in enumerate(groups_of[t]):
+                nc.vector.bn_stats(out=stats[t][:, 1 + n, :], in_=banks_of[t][n][:, cols])
+            all_stats = stats[t][:, 0 : 1 + len(groups_of[t]), :].rearrange("p a s -> p (a s)")
+            nc.vector.bn_aggr(out=mean_var[t][:], in_=all_stats)
+            nc.scalar.activation(out=sd[t][:], in_=mean_var[t][:, 1:2], func=ACT.Sqrt)
+
+        def finish(t, cols, pre, by_vector):
+            piece = result[t][:, cols]
+            if by_vector:
                 nc.vector.scalar_tensor_tensor(
-                    out=result[t][:, cols],
-                    in0=result[t][:, cols],
-                    scalar=sd[:, 0:1],
-                    in1=pre,
-                    op0=ALU.mult,
-                    op1=ALU.add,
+                    out=piece, in0=pre, scalar=rstd[t][:, 0:1], in1=piece, op0=ALU.mult, op1=ALU.add
                 )
-                if n == 0:
-                    nc.vector.tensor_scalar(
-                        out=shift[:], in0=mean_var[:, 0:1], scalar1=rstd[:, 0:1], scalar2=-1.0, op0=ALU.mult, op1=ALU.mult
-                    )
-                nc.scalar.activation(
-                    out=result[t][:, cols], in_=result[t][:, cols], func=ACT.Relu, bias=shift[:, 0:1], scale=rstd[:, 0:1]
+                nc.vector.tensor_scalar(
+                    out=piece, in0=piece, scalar1=shift[t][:, 0:1], scalar2=0.0, op0=ALU.add, op1=ALU.max
                 )
-                nc.sync.dma_start(out=out.rearrange("(p t) h -> p t h", t=B_TILES)[:, t, cols], in_=result[t][:, cols])
+            else:
+                nc.vector.scalar_tensor_tensor(
+                    out=piece, in0=piece, scalar=sd[t][:, 0:1], in1=pre, op0=ALU.mult, op1=ALU.add
+                )
+            if cols.start == 0:
+                nc.vector.tensor_scalar(
+                    out=shift[t][:], in0=mean_var[t][:, 0:1], scalar1=rstd[t][:, 0:1], scalar2=-1.0, op0=ALU.mult, op1=ALU.mult
+                )
+            if not by_vector:
+                nc.scalar.activation(out=piece, in_=piece, func=ACT.Relu, bias=shift[t][:, 0:1], scale=rstd[t][:, 0:1])
+            nc.sync.dma_start(out=out.rearrange("(p t) h -> p t h", t=B_TILES)[:, t, cols], in_=piece)
+
+        statistics(0)
+        for t in range(B_TILES):
+            if t == last:
+                statistics(t)
+            nc.vector.tensor_scalar_add(out=sd[t][:], in0=sd[t][:], scalar1=EPS)
+            nc.vector.reciprocal(out=rstd[t][:], in_=sd[t][:])
+            pieces = [(cols, pre_first[t][:, cols]) for cols in ((first_cols,) if t < last else END_COLS)]
+            for bank, cols in zip(banks_of[t], groups_of[t]):
+                pieces.append((slice(H_HALF + cols.start, H_HALF + cols.stop), bank[:, cols]))
+            for n, (cols, pre) in enumerate(pieces):
+                if t < last - 1 and n == len(pieces) - 1:
+                    statistics(t + 1)
+                finish(t, cols, pre, t == last and n == len(pieces) - 1)

from contextlib import ExitStack

import concourse.mybir as mybir
from concourse.masks import make_identity

F32 = mybir.dt.float32
BF16 = mybir.dt.bfloat16
U32 = mybir.dt.uint32
U8 = mybir.dt.uint8
FP8X4 = mybir.dt.float8_e4m3fn_x4
ALU = mybir.AluOpType
ACT = mybir.ActivationFunctionType

P = 128
PACK = 4
K_PASS = P * PACK
PASS_WORDS = K_PASS // 2
B, H = 512, 1024
B_TILES = B // P
H_HALF = 512
SLAB_ROWS = 512
ROW_TILES = SLAB_ROWS // P
K_TOTAL = 512 + 1024 + 4096
PASSES = K_TOTAL // K_PASS
K_CHUNK = 2 * K_PASS
ACTS = "acts"
CUTS = (((1,), (2,), (2, 2, 2, 2)), ((1,), (2,), (4, 2, 2)))
RAW_BUFS = 8
LAG = 3
EARLY_LAG = 2
RUN = 2
WARM_UP = 5
MU_SLAB = 3
END_COLS = (slice(0, 256), slice(256, 512))
SORTED_PASSES = (4, 6, 8, 10)
SORT_AHEAD = 3
INTERNAL_AFTER = 11
DRIVE_SLABS = (15, 17, 19, 21)
EPS = 0.0001

FLOPS = 2 * B * H * K_TOTAL


def tile_sparsegatedrnncell_pb_kernel(tc, x, hx, sy, internal, W_ih, W_hh, W_sh, mu, out):
    nc = tc.nc
    with ExitStack() as ctx:
        const = ctx.enter_context(tc.tile_pool(name="const", bufs=1))
        keep = ctx.enter_context(tc.tile_pool(name="keep", bufs=1))
        raw_pool = ctx.enter_context(tc.tile_pool(name="raw_pool", bufs=RAW_BUFS))
        long_pool = ctx.enter_context(tc.tile_pool(name="long_pool", bufs=1))
        stage = ctx.enter_context(tc.tile_pool(name="stage", bufs=3))
        sorted_pool = ctx.enter_context(tc.tile_pool(name="sorted_pool", bufs=SORT_AHEAD + 1))
        banks = ctx.enter_context(tc.psum_pool(name="banks", bufs=4))
        sums = ctx.enter_context(tc.psum_pool(name="sums", bufs=4))
        ctx.enter_context(tc.manual_schedule())

        loads = []
        for part, cuts in enumerate(CUTS):
            first = 0
            for (act, weight), stream_cuts in zip(((x, W_ih), (hx, W_hh), (sy, W_sh)), cuts):
                k0 = 0
                for passes in stream_cuts:
                    if part == 0:
                        loads.append((ACTS, first, passes, act, 0, k0))
                    loads.append((part, first, passes, weight, part * H_HALF, k0))
                    first += passes
                    k0 += passes * K_PASS
        raw = {}
        internal_sb = const.tile([P, B_TILES, H], BF16)

        def issue_loads(count):
            for what, first, per_load, source, row0, k0 in loads[len(raw) : len(raw) + count]:
                width = per_load * K_PASS
                if per_load > 2:
                    rows = long_pool.tile([P, ROW_TILES * width], BF16, name="long_rows", tag="long_rows")
                else:
                    rows = raw_pool.tile([P, ROW_TILES * K_CHUNK], BF16, name="rows", tag="rows")
                nc.sync.dma_start(
                    out=rows[:, 0 : ROW_TILES * width].rearrange("p (j k) -> p j k", j=ROW_TILES),
                    in_=source[row0 : row0 + SLAB_ROWS, k0 : k0 + width].rearrange("(p j) k -> p j k", j=ROW_TILES),
                )
                raw[(what, first)] = rows
                if len(raw) == INTERNAL_AFTER:
                    nc.sync.dma_start(out=internal_sb[:], in_=internal.rearrange("(p t) h -> p t h", t=B_TILES))

        ones = const.tile([P, H_HALF], BF16)
        nc.vector.memset(ones[:], 1.0)
        mu_rows = const.tile([P, H], BF16)
        nc.vector.memset(mu_rows[:], 0.0)
        issue_loads(2)
        nc.sync.dma_start(out=mu_rows[0:1, :], in_=mu.rearrange("(o h) -> o h", o=1))
        issue_loads(RAW_BUFS - 2)

        warm = const.tile([P, 1], F32)
        nc.vector.memset(warm[:], 1.0)
        nc.scalar.activation(out=warm[:], in_=warm[:], func=ACT.Sqrt)
        ident = const.tile([P, P], F32)
        make_identity(nc, ident[:])
        mu_all = const.tile([P, H], BF16)

        def keep_busy(count):
            unread = banks.tile([P, H_HALF], F32, tag="bank")
            for n in range(count):
                nc.tensor.matmul(out=unread[:], lhsT=ones[:, 0:P], rhs=ones[:], start=True, stop=True)

        def spread_mu(cols):
            spread = banks.tile([P, H_HALF], F32, tag="bank")
            nc.tensor.matmul(out=spread[:], lhsT=ones[:, 0:P], rhs=mu_rows[:, cols], start=True, stop=True)
            nc.vector.tensor_copy(out=mu_all[:, cols], in_=spread[:])

        a_codes = keep.tile([P, PASSES, B], U32, align_bytes=64)
        a_scales = keep.tile([P, PASSES, B], U8, align_bytes=64)
        w_codes = keep.tile([P, PASSES, H], U32, align_bytes=64)
        w_scales = keep.tile([P, PASSES, H], U8, align_bytes=64)

        def sort_slab(rows, per_load, local):
            ordered = sorted_pool.tile([P, ROW_TILES * K_PASS], BF16, align_bytes=64, tag="ordered")
            loaded = rows[:, 0 : ROW_TILES * per_load * K_PASS].rearrange("p (j l k) -> p j l k", j=ROW_TILES, l=per_load)
            nc.vector.tensor_copy(
                out=ordered[:].rearrange("p (u j q e) -> p j q u e", u=2, j=ROW_TILES, e=16),
                in_=loaded[:, :, local, :].rearrange("p j (q u e) -> p j q u e", u=2, e=16),
            )
            return ordered

        def transpose_slab(rows, per_load, local, ordered, in_row_order):
            words = (rows if ordered is None else ordered)[:].bitcast(F32)
            grouped = stage.tile([P, SLAB_ROWS * PACK], BF16, align_bytes=64, tag="grouped")
            words_out = grouped[:].bitcast(F32)
            for pair in range(ROW_TILES // 2):
                bank = banks.tile([P, 2, 2, P], F32, tag="bank")
                for j in range(2):
                    for u in range(2):
                        row_tile = 2 * pair + j
                        if ordered is None:
                            first = (row_tile * per_load + local) * PASS_WORDS
                            these = words[:, first + u : first + PASS_WORDS : 2]
                        else:
                            first = (u * ROW_TILES + row_tile) * P
                            these = words[:, first : first + P]
                        nc.tensor.transpose(bank[:, j, u, :], these, ident[:])
                two = slice(2 * pair, 2 * pair + 2)
                if in_row_order:
                    nc.scalar.copy(
                        out=words_out.rearrange("p (r j u) -> p r j u", j=ROW_TILES, u=2)[:, :, two, :],
                        in_=bank[:].rearrange("p j u r -> p r j u"),
                    )
                else:
                    nc.scalar.copy(
                        out=words_out.rearrange("p (j r u) -> p j r u", j=ROW_TILES, u=2)[:, two, :, :],
                        in_=bank[:].rearrange("p j u r -> p j r u"),
                    )
            return grouped

        def mx_pass(acc, t, half, c, cols=slice(0, H_HALF)):
            b_cols = slice(t * P, (t + 1) * P)
            h_cols = slice(half * H_HALF + cols.start, half * H_HALF + cols.stop)
            nc.tensor.matmul_mx(
                out=acc[:, cols],
                lhsT=a_codes[:, c, b_cols].bitcast(FP8X4),
                lhsT_scale=a_scales[:, c, b_cols],
                rhs=w_codes[:, c, h_cols].bitcast(FP8X4),
                rhs_scale=w_scales[:, c, h_cols],
                start=(c == 0),
                stop=(c == PASSES - 1),
            )

        first_cols = slice(0, H_HALF)
        second_cols = slice(H_HALF, H)
        slabs = []
        ready = {}
        held = []
        for what, first, passes, source, row0, k0 in loads:
            held.append([(what, first, passes, local) for local in range(passes)])
            if what == ACTS:
                continue
            if len(held) == 2 and source is W_sh:
                order = [which[local] for local in range(passes) for which in held]
            else:
                order = [slab for which in held for slab in which]
            held = []
            for which, start, count, local in order:
                c = start + local
                if which == ACTS:
                    codes, scales = a_codes[:, c, :], a_scales[:, c, :]
                else:
                    cols = (first_cols, second_cols)[which]
                    codes, scales = w_codes[:, c, cols], w_scales[:, c, cols]
                    ready[(which, c)] = len(slabs)
                slabs.append(((which, start), count, local, local == count - 1, c, codes, scales))
        part1_slabs = PASSES * 2

        acc = {(0, t): sums.tile([P, H_HALF], F32, name="acc_first%d" % t, tag="acc") for t in range(B_TILES)}
        todo = {0: [(c, t) for c in range(PASSES) for t in range(B_TILES)], 1: [(c, t) for t in range(B_TILES - 1) for c in range(PASSES)]}
        result = [keep.tile([P, H], F32, name="result%d" % t) for t in range(B_TILES)]
        pre_first = [keep.tile([P, H_HALF], F32, name="pre_first%d" % t) for t in range(B_TILES)]
        stats = [keep.tile([P, 1 + len(END_COLS), 6], F32, name="stats%d" % t) for t in range(B_TILES)]
        summed = []

        def run_passes(slab, count):
            half = 0 if todo[0] else 1
            possible = [(c, t) for c, t in todo[half] if ready[(half, c)] + (LAG if slab > 6 else EARLY_LAG) <= slab]
            for c, t in possible[:count]:
                todo[half].remove((c, t))
                mx_pass(acc[(half, t)], t, half, c)
                if half == 0 and c == PASSES - 1:
                    nc.vector.tensor_copy(out=pre_first[t][:], in_=acc[(0, t)][:])
                    acc[(1, t)] = sums.tile([P, H_HALF], F32, name="acc_second%d" % t, tag="acc")
                    summed.append(t)
            return len(possible[:count])

        keep_busy(WARM_UP)
        ordered = {}
        for i, (key, per_load, local, last_of_load, c_slab, codes, scales) in enumerate(slabs):
            ahead = i + SORT_AHEAD
            if ahead < len(slabs):
                soon, soon_passes, soon_local, last, soon_pass = slabs[ahead][0:5]
                if soon_pass in SORTED_PASSES:
                    ordered[ahead] = sort_slab(raw[soon], soon_passes, soon_local)
            grouped = transpose_slab(raw[key], per_load, local, ordered.get(i), key[0] != ACTS)
            if last_of_load and len(raw) < len(loads):
                issue_loads(1)
            old_sums = list(summed)
            if i == MU_SLAB:
                spread_mu(first_cols)
                spread_mu(second_cols)
            elif run_passes(i, RUN) == 0:
                keep_busy(RUN)
            nc.vector.quantize_mx(out=codes.bitcast(FP8X4), scales=scales, in_=grouped[:])
            if i in DRIVE_SLABS:
                t = DRIVE_SLABS.index(i)
                nc.vector.tensor_tensor(out=result[t][:], in0=internal_sb[:, t, :], in1=mu_all[:], op=ALU.add)
            if old_sums:
                t = summed.pop(0)
                nc.vector.bn_stats(out=stats[t][:, 0, :], in_=pre_first[t][:])
        assert len(raw) == len(loads) and not todo[0] and not summed

        for i in range(len(slabs), len(slabs) + LAG):
            run_passes(i, RUN)
        last = B_TILES - 1
        for t in range(last):
            run_passes(len(slabs) + LAG, PASSES)
        banks_of = {t: [acc[(1, t)]] for t in range(B_TILES)}
        banks_of[last] += [banks.tile([P, H_HALF], F32, name="acc_end", tag="bank") for cols in END_COLS[1:]]
        groups_of = {t: (slice(0, H_HALF),) for t in range(last)}
        groups_of[last] = END_COLS
        for bank, cols in zip(banks_of[last], END_COLS):
            for c in range(PASSES):
                mx_pass(bank, last, 1, c, cols)

        mean_var = [keep.tile([P, 2], F32, name="mean_var%d" % t) for t in range(B_TILES)]
        sd = [keep.tile([P, 1], F32, name="sd%d" % t) for t in range(B_TILES)]
        rstd = [keep.tile([P, 1], F32, name="rstd%d" % t) for t in range(B_TILES)]
        shift = [keep.tile([P, 1], F32, name="shift%d" % t) for t in range(B_TILES)]

        def statistics(t):
            for n, cols in enumerate(groups_of[t]):
                nc.vector.bn_stats(out=stats[t][:, 1 + n, :], in_=banks_of[t][n][:, cols])
            all_stats = stats[t][:, 0 : 1 + len(groups_of[t]), :].rearrange("p a s -> p (a s)")
            nc.vector.bn_aggr(out=mean_var[t][:], in_=all_stats)
            nc.scalar.activation(out=sd[t][:], in_=mean_var[t][:, 1:2], func=ACT.Sqrt)

        def finish(t, cols, pre, by_vector):
            piece = result[t][:, cols]
            if by_vector:
                nc.vector.scalar_tensor_tensor(
                    out=piece, in0=pre, scalar=rstd[t][:, 0:1], in1=piece, op0=ALU.mult, op1=ALU.add
                )
                nc.vector.tensor_scalar(
                    out=piece, in0=piece, scalar1=shift[t][:, 0:1], scalar2=0.0, op0=ALU.add, op1=ALU.max
                )
            else:
                nc.vector.scalar_tensor_tensor(
                    out=piece, in0=piece, scalar=sd[t][:, 0:1], in1=pre, op0=ALU.mult, op1=ALU.add
                )
            if cols.start == 0:
                nc.vector.tensor_scalar(
                    out=shift[t][:], in0=mean_var[t][:, 0:1], scalar1=rstd[t][:, 0:1], scalar2=-1.0, op0=ALU.mult, op1=ALU.mult
                )
            if not by_vector:
                nc.scalar.activation(out=piece, in_=piece, func=ACT.Relu, bias=shift[t][:, 0:1], scale=rstd[t][:, 0:1])
            nc.sync.dma_start(out=out.rearrange("(p t) h -> p t h", t=B_TILES)[:, t, cols], in_=piece)

        statistics(0)
        for t in range(B_TILES):
            if t == last:
                statistics(t)
            nc.vector.tensor_scalar_add(out=sd[t][:], in0=sd[t][:], scalar1=EPS)
            nc.vector.reciprocal(out=rstd[t][:], in_=sd[t][:])
            pieces = [(cols, pre_first[t][:, cols]) for cols in ((first_cols,) if t < last else END_COLS)]
            for bank, cols in zip(banks_of[t], groups_of[t]):
                pieces.append((slice(H_HALF + cols.start, H_HALF + cols.stop), bank[:, cols]))
            for n, (cols, pre) in enumerate(pieces):
                if t < last - 1 and n == len(pieces) - 1:
                    statistics(t + 1)
                finish(t, cols, pre, t == last and n == len(pieces) - 1)
